import numpy as np
import ml_dtypes


def mxq(x, axis, fmt="e4m3"):
    dtype, down = {"e4m3": (ml_dtypes.float8_e4m3fn, 7), "e5m2": (ml_dtypes.float8_e5m2, 14)}[fmt]
    v = np.moveaxis(np.asarray(x, np.float32).astype(ml_dtypes.bfloat16).astype(np.float64), axis, -1)
    blocks = v.reshape(v.shape[:-1] + (-1, 32))
    amax = np.abs(blocks).max(-1, keepdims=True)
    byte = np.maximum(np.where(amax > 0, np.frexp(amax)[1] - 1 + 127, 0) - down, 1)
    scale = np.exp2(byte - 127.0)
    codes = (blocks / scale).astype(np.float32).astype(dtype).astype(np.float64)
    return np.moveaxis((codes * scale).reshape(v.shape), -1, axis)


WIDE = False


def mx_kscale(k):
    if not WIDE:
        return np.ones(k)
    levels = np.array([10, -10, 5, -5, 0])
    if k % 512:
        return np.exp2(np.random.permutation(np.resize(levels, k // 32))).repeat(32)
    a = np.empty((k // 512, 16))
    for p in range(k // 512):
        a[p, :8] = np.random.permutation(np.resize(levels, 8))
        for g in range(8):
            far = levels[np.abs(levels - a[p, g]) >= 10]
            a[p, g + 8] = far[np.random.randint(len(far))]
    return np.exp2(a.ravel()).repeat(32)


BF16 = ml_dtypes.bfloat16


def bf(x):
    return np.asarray(x, np.float32).astype(BF16)


def f64(x):
    return np.asarray(x).astype(np.float64)


B, S, DIM, H, HD = 4, 128, 2048, 16, 128
E = H * HD


def rope_tables():
    inv_freq = 1.0 / (10000.0 ** (np.arange(0, HD, 2) / HD))
    freqs = np.outer(np.arange(S), inv_freq)
    emb = np.concatenate([freqs, freqs], axis=-1)
    return np.cos(emb)[None, None], np.sin(emb)[None, None]


def rotate_half(x):
    x1, x2 = np.split(x, 2, axis=-1)
    return np.concatenate([-x2, x1], axis=-1)


def setup_inputs():
    s = mx_kscale(DIM)
    cos, sin = rope_tables()
    return {"query": bf(np.random.standard_normal((B, S, DIM)) * s),
            "wq": bf(np.random.standard_normal((E, DIM)) / np.sqrt(DIM) / s),
            "bq": bf(np.random.standard_normal(E) * 0.1),
            "cos": bf(cos), "sin": bf(sin)}


def core(query, wq, bq, cos, sin):
    q = (mxq(f64(query), 2, "e4m3") @ mxq(f64(wq), 1, "e4m3").T) + f64(bq)
    q = q.reshape(B, S, H, HD).transpose(0, 2, 1, 3)
    return q * f64(cos) + rotate_half(q) * f64(sin)


def e4m3fn_bytes(y):
    return np.clip(np.asarray(y, np.float64), -448.0, 448.0).astype(np.float32).astype(ml_dtypes.float8_e4m3fn).view(np.uint8)


def reference(query, wq, bq, cos, sin):
    out = core(query, wq, bq, cos, sin)
    s = np.max(np.abs(out), axis=-1, keepdims=True) / 448.0
    return out, e4m3fn_bytes(out / s)

@@ -1,0 +1,300 @@
+from contextlib import ExitStack
+
+import concourse.mybir as mybir
+from concourse.masks import make_identity
+
+B, S, DIM, H, HD = 4, 128, 2048, 16, 128
+FLOPS = 2 * B * S * DIM * H * HD
+
+F32 = mybir.dt.float32
+BF16 = mybir.dt.bfloat16
+U32 = mybir.dt.uint32
+U8 = mybir.dt.uint8
+FP8X4 = mybir.dt.float8_e4m3fn_x4
+FP8 = mybir.dt.float8_e4m3fn
+ALU = mybir.AluOpType
+ACT = mybir.ActivationFunctionType
+AX = mybir.AxisListType
+
+P = 128
+NG = 4
+ROWS = 256
+NPAIR = 8
+HALF = 64
+
+
+def tile_attention_pa_kernel(tc, query, wq, bq, cos, sin, out_0, out_1):
+    nc = tc.nc
+    with ExitStack() as ctx:
+        const = ctx.enter_context(tc.tile_pool(name="const", bufs=1))
+        rawp = ctx.enter_context(tc.tile_pool(name="rawp", bufs=20))
+        grp = ctx.enter_context(tc.tile_pool(name="grp", bufs=3))
+        qcp = ctx.enter_context(tc.tile_pool(name="qcp", bufs=2))
+        wcp = ctx.enter_context(tc.tile_pool(name="wcp", bufs=4))
+        prod = ctx.enter_context(tc.tile_pool(name="prod", bufs=2))
+        work = ctx.enter_context(tc.tile_pool(name="work", bufs=4))
+        tpp = ctx.enter_context(tc.psum_pool(name="tpp", bufs=4))
+        accp = ctx.enter_context(tc.psum_pool(name="accp", bufs=2))
+        obp = ctx.enter_context(tc.psum_pool(name="obp", bufs=2))
+        ctx.enter_context(tc.manual_schedule())
+
+        zeros = const.tile([P, 1], F32, name="zeros")
+        nc.vector.memset(zeros[:], 0.0)
+        dz = const.tile([P, 512], BF16, name="dz")
+        nc.vector.memset(dz[:], 0.0)
+        zb = const.tile([P, P], BF16, name="zb")
+        nc.vector.memset(zb[:], 0.0)
+        bq4 = bq.rearrange("(i hl f j) -> f i hl j", i=NPAIR, hl=2, f=2, j=HALF)
+        cosb = const.tile([P, HD], BF16, name="cosb")
+        sinb = const.tile([P, HD], BF16, name="sinb")
+        warm = const.tile([P, 1], F32, name="warm")
+        nc.scalar.activation(out=warm[:], in_=zeros[:], func=ACT.Identity, bias=zeros[:, 0:1], scale=zeros[:, 0:1])
+        identf = const.tile([P, P], F32, name="identf")
+        make_identity(nc, identf[:])
+        identb = const.tile([P, P], BF16, name="identb")
+        make_identity(nc, identb[:])
+
+        order = [("w", 0), ("q", 0), ("q", 1)] + [("w", i) for i in range(1, NPAIR)]
+        raws = {}
+        for key in order:
+            for j in range(2):
+                raw = rawp.tile([P, DIM], BF16, name="raw", tag="raw")
+                if key[0] == "q":
+                    src = query[2 * key[1] + j]
+                else:
+                    src = wq[ROWS * key[1] + P * j : ROWS * key[1] + P * (j + 1), :]
+                pieces = NG if (key, j) == (("w", 0), 0) else 1
+                step = DIM // pieces
+                for c in range(pieces):
+                    nc.sync.dma_start(out=raw[:, step * c : step * (c + 1)], in_=src[:, step * c : step * (c + 1)])
+                raws[(key, j)] = raw
+            if key == ("w", 0):
+                nc.sync.dma_start(out=cosb[:], in_=cos[0, 0])
+                nc.sync.dma_start(out=sinb[:], in_=sin[0, 0])
+                for f in range(2):
+                    nc.sync.dma_start(out=zb[NPAIR * f : NPAIR * (f + 1), :].rearrange("p (hl j) -> p hl j", hl=2), in_=bq4[f])
+
+        xt = const.tile([P, 4, P], BF16, name="xt")
+
+        def dup(k, src, lo, sign):
+            nc.vector.tensor_scalar(
+                out=xt[:, k, :].rearrange("p (hl j) -> p hl j", hl=2),
+                in0=src[:, lo : lo + HALF].unsqueeze(1).to_broadcast([P, 2, HALF]),
+                scalar1=sign, scalar2=None, op0=ALU.mult)
+
+        tabs = const.tile([P, 4, P], F32, name="tabs")
+        bt = const.tile([P, 2 * NPAIR], F32, name="bt")
+
+        def tables():
+            dup(0, cosb, 0, 1.0)
+            dup(1, sinb, 0, -1.0)
+            dup(2, cosb, HALF, 1.0)
+            dup(3, sinb, HALF, 1.0)
+            small = tpp.tile([P, 5, P], BF16, name="tp", tag="tp")
+            for k in range(4):
+                nc.tensor.transpose(small[:, k, :], xt[:, k, :], identb[:])
+            nc.tensor.transpose(small[:, 4, :], zb[:], identb[:])
+            nc.vector.tensor_copy(out=tabs[:], in_=small[:, 0:4, :])
+            nc.vector.tensor_copy(out=bt[:], in_=small[:, 4, 0 : 2 * NPAIR])
+
+        groupeds, codes = {}, {}
+
+        def transposes(key, j):
+            if j == 0:
+                grouped = grp.tile([P, NG * ROWS * 4], BF16, name="grouped", tag="grouped", align_bytes=64)
+                groupeds[key] = grouped
+            words = raws[(key, j)][:].bitcast(F32)
+            gwords = groupeds[key][:].bitcast(F32)
+            for gh in range(2):
+                tp = tpp.tile([P, 4, P], F32, name="tp", tag="tp")
+                for gl in range(2):
+                    for u in range(2):
+                        base = 256 * (2 * gh + gl)
+                        slot = 2 * gl + u if key[0] == "q" else 2 * u + gl
+                        nc.tensor.transpose(tp[:, slot, :], words[:, base + u : base + 256 : 2], identf[:])
+                if key[0] == "q":
+                    nc.scalar.copy(
+                        out=gwords.rearrange("p (g r u) -> p g r u", g=NG, u=2)[:, 2 * gh : 2 * gh + 2, P * j : P * (j + 1), :],
+                        in_=tp[:].rearrange("p (gl u) r -> p gl r u", u=2))
+                else:
+                    nc.scalar.copy(
+                        out=gwords.rearrange("p (gh y hl j u) -> p gh y hl j u", gh=2, y=4, hl=2, u=2)[:, gh, :, j, :, :],
+                        in_=tp[:].rearrange("p q r -> p (q r)").rearrange("p (u y j) -> p y j u", u=2, y=4))
+
+        def quantize(key, lo, hi):
+            if key not in codes:
+                pool = qcp if key[0] == "q" else wcp
+                cd = pool.tile([P, NG * ROWS], U32, name="cd" + key[0], tag="cd" + key[0], align_bytes=64)
+                sc = pool.tile([P, NG * ROWS], U8, name="sc" + key[0], tag="sc" + key[0], align_bytes=64)
+                codes[key] = (cd, sc)
+            cd, sc = codes[key]
+            nc.vector.quantize_mx(
+                out=cd[:, ROWS * lo : ROWS * hi].bitcast(FP8X4), scales=sc[:, ROWS * lo : ROWS * hi],
+                in_=groupeds[key][:, 4 * ROWS * lo : 4 * ROWS * hi])
+
+        accs, prods, obs, outs, rcs = {}, {}, {}, {}, {}
+
+        def matmuls(i, f, bp):
+            if (i, f) not in accs:
+                acc = accp.tile([P, 512], F32, name="acc", tag="acc")
+                accs[(i, f)] = acc
+            acc = accs[(i, f)]
+            qc, qs = codes[("q", bp)]
+            wc, ws = codes[("w", i)]
+            for g in range(NG):
+                m0 = g * ROWS + f * P
+                nc.tensor.matmul_mx(
+                    out=acc[:, ROWS * bp : ROWS * (bp + 1)],
+                    lhsT=wc[:, m0 : m0 + P].bitcast(FP8X4), lhsT_scale=ws[:, m0 : m0 + P],
+                    rhs=qc[:, g * ROWS : (g + 1) * ROWS].bitcast(FP8X4), rhs_scale=qs[:, g * ROWS : (g + 1) * ROWS],
+                    start=(g == 0), stop=(g == NG - 1))
+
+        SIDE = (0, 1, 1, 0)
+
+        def product(i, k, b0, b1):
+            if (i, k) not in prods:
+                pt = prod.tile([P, 512], F32, name="pt" + str(k), tag="pt" + str(k))
+                prods[(i, k)] = pt
+            f = SIDE[k]
+            nc.vector.scalar_tensor_tensor(
+                out=prods[(i, k)][:, P * b0 : P * b1].rearrange("p (b s) -> p b s", s=S),
+                in0=accs[(i, f)][:, P * b0 : P * b1].rearrange("p (b s) -> p b s", s=S),
+                scalar=bt[:, NPAIR * f + i : NPAIR * f + i + 1],
+                in1=tabs[:, k, :].unsqueeze(1).to_broadcast([P, b1 - b0, S]),
+                op0=ALU.add, op1=ALU.mult)
+
+        def products(i, b0, b1):
+            for k in (0, 3, 1, 2):
+                product(i, k, b0, b1)
+
+        summed = {}
+
+        def sums(i, eng, b0, b1):
+            for f in range(2):
+                eng.tensor_tensor(out=prods[(i, 2 * f)][:, P * b0 : P * b1], in0=prods[(i, 2 * f)][:, P * b0 : P * b1],
+                                  in1=prods[(i, 2 * f + 1)][:, P * b0 : P * b1], op=ALU.add)
+            summed[i] = True
+
+        def back(i, bp):
+            ob = obp.tile([P, 512], F32, name="ob", tag="ob")
+            nt = 1 if i in summed else 2
+            for f in range(2):
+                for bl in range(2):
+                    b = 2 * bp + bl
+                    c0 = ROWS * f + P * bl
+                    for t in range(nt):
+                        nc.tensor.matmul(out=ob[:, c0 : c0 + P], lhsT=prods[(i, 2 * f + t)][:, P * b : P * (b + 1)], rhs=identf[:],
+                                         is_transpose=True, start=(t == 0), stop=(t == nt - 1))
+            o = work.tile([P, 512], F32, name="o", tag="o", bufs=5)
+            nc.scalar.copy(out=o[:].rearrange("p (x f j) -> p x f j", f=2, j=HALF),
+                           in_=ob[:].rearrange("p (f x j) -> p x f j", f=2, j=HALF))
+            outs[(i, bp)] = o
+            for bl in range(2):
+                nc.sync.dma_start(
+                    out=out_0[2 * bp + bl, 2 * i : 2 * i + 2].rearrange("h s d -> s h d"),
+                    in_=o[:, ROWS * bl : ROWS * (bl + 1)].rearrange("p (h d) -> p h d", d=HD))
+
+        def bytes_out(i, bp, shared=False):
+            o = outs[(i, bp)]
+            am = work.tile([P, 4], F32, name="am", tag="am")
+            nc.vector.tensor_reduce(out=am[:], in_=o[:].rearrange("p (x d) -> p x d", d=HD), axis=AX.X, op=ALU.max,
+                                    apply_absolute_value=True)
+            rc = work.tile([P, 4], F32, name="rc", tag="rc")
+            nc.vector.reciprocal(out=rc[:], in_=am[:])
+            rs = work.tile([P, 4], F32, name="rs", tag="rs")
+            if shared:
+                nc.vector.tensor_scalar(out=rs[:], in0=rc[:], scalar1=448.0, scalar2=None, op0=ALU.mult)
+            else:
+                nc.scalar.activation(out=rs[:], in_=rc[:], func=ACT.Copy, scale=448.0)
+            f8 = work.tile([P, 512], FP8, name="f8", tag="f8")
+            for x in range(4):
+                if shared and x < 2:
+                    nc.vector.tensor_scalar(out=f8[:, HD * x : HD * (x + 1)], in0=o[:, HD * x : HD * (x + 1)],
+                                            scalar1=rs[:, x : x + 1], scalar2=None, op0=ALU.mult, saturate=False)
+                else:
+                    nc.scalar.activation(out=f8[:, HD * x : HD * (x + 1)], in_=o[:, HD * x : HD * (x + 1)], func=ACT.Identity,
+                                         bias=zeros[:, 0:1], scale=rs[:, x : x + 1], saturate=False)
+            for bl in range(2):
+                nc.sync.dma_start(
+                    out=out_1[2 * bp + bl, 2 * i : 2 * i + 2].rearrange("h s d -> s h d"),
+                    in_=f8[:, ROWS * bl : ROWS * (bl + 1)].bitcast(U8).rearrange("p (h d) -> p h d", d=HD))
+
+        q0, q1 = ("q", 0), ("q", 1)
+        dm = obp.tile([P, 512], F32, name="ob", tag="ob")
+
+        def keep_warm(n):
+            for r in range(n):
+                nc.tensor.matmul(out=dm[:], lhsT=dz[:, 0:P], rhs=dz[:], start=True, stop=True)
+
+        def w(i):
+            return ("w", i)
+
+        keep_warm(4)
+        transposes(w(0), 0)
+        keep_warm(1)
+        transposes(w(0), 1)
+        keep_warm(1)
+        tables()
+        transposes(q0, 0)
+        keep_warm(1)
+        transposes(q0, 1)
+        keep_warm(1)
+        quantize(w(0), 0, 2)
+        quantize(w(0), 2, 4)
+        quantize(q0, 0, 2)
+        quantize(q0, 2, 4)
+        transposes(q1, 0)
+        matmuls(0, 0, 0)
+        matmuls(0, 1, 0)
+        transposes(q1, 1)
+        keep_warm(1)
+        products(0, 0, 2)
+        sums(0, nc.vector, 0, 2)
+        quantize(q1, 0, 2)
+        quantize(q1, 2, 4)
+        transposes(w(1), 0)
+        keep_warm(1)
+        transposes(w(1), 1)
+        matmuls(0, 0, 1)
+        matmuls(0, 1, 1)
+        back(0, 0)
+        quantize(w(1), 0, NG)
+        products(0, 2, 4)
+        sums(0, nc.vector, 2, 4)
+        transposes(w(2), 0)
+        transposes(w(2), 1)
+        bytes_out(0, 0)
+
+        for i in range(1, NPAIR):
+            last = i == NPAIR - 1
+            if not last:
+                quantize(w(i + 1), 0, NG)
+            if last:
+                for bp in range(2):
+                    for f in range(2):
+                        matmuls(i, f, bp)
+            else:
+                for f in range(2):
+                    for bp in range(2):
+                        matmuls(i, f, bp)
+            if last:
+                products(i, 0, 2)
+            else:
+                products(i, 0, 4)
+                sums(i, nc.gpsimd, 0, 4)
+            if i > 1:
+                back(i - 1, 0)
+            back(i - 1, 1)
+            if last:
+                products(i, 2, 4)
+            if i + 2 < NPAIR:
+                transposes(w(i + 2), 0)
+                transposes(w(i + 2), 1)
+            if last:
+                back(i, 0)
+                back(i, 1)
+            if i > 1:
+                bytes_out(i - 1, 0)
+            bytes_out(i - 1, 1)
+        bytes_out(NPAIR - 1, 0)
+        bytes_out(NPAIR - 1, 1, True)

@@ -68,11 +68,11 @@ def tile_attention_pa_kernel(tc, query, wq, bq, cos, sin, out_0, out_1):
                 for c in range(pieces):
                     nc.sync.dma_start(out=raw[:, step * c : step * (c + 1)], in_=src[:, step * c : step * (c + 1)])
                 raws[(key, j)] = raw
-            if key == ("w", 0):
-                nc.sync.dma_start(out=cosb[:], in_=cos[0, 0])
-                nc.sync.dma_start(out=sinb[:], in_=sin[0, 0])
+            if key == ("q", 0):
                 for f in range(2):
                     nc.sync.dma_start(out=zb[NPAIR * f : NPAIR * (f + 1), :].rearrange("p (hl j) -> p hl j", hl=2), in_=bq4[f])
+                nc.sync.dma_start(out=cosb[:], in_=cos[0, 0])
+                nc.sync.dma_start(out=sinb[:], in_=sin[0, 0])
 
         xt = const.tile([P, 4, P], BF16, name="xt")
 
@@ -234,13 +234,13 @@ def tile_attention_pa_kernel(tc, query, wq, bq, cos, sin, out_0, out_1):
         keep_warm(1)
         transposes(w(0), 1)
         keep_warm(1)
-        tables()
         transposes(q0, 0)
-        keep_warm(1)
-        transposes(q0, 1)
         keep_warm(1)
         quantize(w(0), 0, 2)
         quantize(w(0), 2, 4)
+        transposes(q0, 1)
+        keep_warm(1)
+        tables()
         quantize(q0, 0, 2)
         quantize(q0, 2, 4)
         transposes(q1, 0)

@@ -164,7 +164,7 @@ def tile_attention_pa_kernel(tc, query, wq, bq, cos, sin, out_0, out_1):
                 op0=ALU.add, op1=ALU.mult)
 
         def products(i, b0, b1):
-            for k in (0, 3, 1, 2):
+            for k in ((0, 1, 3, 2) if 0 < i < NPAIR - 1 else (0, 3, 1, 2)):
                 product(i, k, b0, b1)
 
         summed = {}

@@ -208,7 +208,7 @@ def tile_attention_pa_kernel(tc, query, wq, bq, cos, sin, out_0, out_1):
                 nc.scalar.activation(out=rs[:], in_=rc[:], func=ACT.Copy, scale=448.0)
             f8 = work.tile([P, 512], FP8, name="f8", tag="f8")
             for x in range(4):
-                if shared and x < 2:
+                if shared and x < 3:
                     nc.vector.tensor_scalar(out=f8[:, HD * x : HD * (x + 1)], in0=o[:, HD * x : HD * (x + 1)],
                                             scalar1=rs[:, x : x + 1], scalar2=None, op0=ALU.mult, saturate=False)
                 else:
@@ -218,6 +218,30 @@ def tile_attention_pa_kernel(tc, query, wq, bq, cos, sin, out_0, out_1):
                 nc.sync.dma_start(
                     out=out_1[2 * bp + bl, 2 * i : 2 * i + 2].rearrange("h s d -> s h d"),
                     in_=f8[:, ROWS * bl : ROWS * (bl + 1)].bitcast(U8).rearrange("p (h d) -> p h d", d=HD))
+
+        def bytes_both(i):
+            ams, rss = [], []
+            for bp in range(2):
+                am = work.tile([P, 4], F32, name="am", tag="am")
+                nc.vector.tensor_reduce(out=am[:], in_=outs[(i, bp)][:].rearrange("p (x d) -> p x d", d=HD), axis=AX.X, op=ALU.max,
+                                        apply_absolute_value=True)
+                ams.append(am)
+            for bp in range(2):
+                rc = work.tile([P, 4], F32, name="rc", tag="rc")
+                nc.vector.reciprocal(out=rc[:], in_=ams[bp][:])
+                rs = work.tile([P, 4], F32, name="rs", tag="rs")
+                nc.scalar.activation(out=rs[:], in_=rc[:], func=ACT.Copy, scale=448.0)
+                rss.append(rs)
+            for bp in range(2):
+                o = outs[(i, bp)]
+                f8 = work.tile([P, 512], FP8, name="f8", tag="f8")
+                for x in range(4):
+                    nc.scalar.activation(out=f8[:, HD * x : HD * (x + 1)], in_=o[:, HD * x : HD * (x + 1)], func=ACT.Identity,
+                                         bias=zeros[:, 0:1], scale=rss[bp][:, x : x + 1], saturate=False)
+                for bl in range(2):
+                    nc.sync.dma_start(
+                        out=out_1[2 * bp + bl, 2 * i : 2 * i + 2].rearrange("h s d -> s h d"),
+                        in_=f8[:, ROWS * bl : ROWS * (bl + 1)].bitcast(U8).rearrange("p (h d) -> p h d", d=HD))
 
         q0, q1 = ("q", 0), ("q", 1)
         dm = obp.tile([P, 512], F32, name="ob", tag="ob")
@@ -294,7 +318,8 @@ def tile_attention_pa_kernel(tc, query, wq, bq, cos, sin, out_0, out_1):
                 back(i, 0)
                 back(i, 1)
             if i > 1:
-                bytes_out(i - 1, 0)
-            bytes_out(i - 1, 1)
+                bytes_both(i - 1)
+            else:
+                bytes_out(i - 1, 1)
         bytes_out(NPAIR - 1, 0)
         bytes_out(NPAIR - 1, 1, True)

@@ -169,16 +169,16 @@ def tile_attention_pa_kernel(tc, query, wq, bq, cos, sin, out_0, out_1):
 
         summed = {}
 
-        def sums(i, eng, b0, b1):
-            for f in range(2):
+        def sums(i, eng, b0, b1, halves=(0, 1)):
+            for f in halves:
                 eng.tensor_tensor(out=prods[(i, 2 * f)][:, P * b0 : P * b1], in0=prods[(i, 2 * f)][:, P * b0 : P * b1],
                                   in1=prods[(i, 2 * f + 1)][:, P * b0 : P * b1], op=ALU.add)
-            summed[i] = True
+                summed[(i, f)] = True
 
         def back(i, bp):
             ob = obp.tile([P, 512], F32, name="ob", tag="ob")
-            nt = 1 if i in summed else 2
             for f in range(2):
+                nt = 1 if (i, f) in summed else 2
                 for bl in range(2):
                     b = 2 * bp + bl
                     c0 = ROWS * f + P * bl
@@ -305,7 +305,7 @@ def tile_attention_pa_kernel(tc, query, wq, bq, cos, sin, out_0, out_1):
                 products(i, 0, 2)
             else:
                 products(i, 0, 4)
-                sums(i, nc.gpsimd, 0, 4)
+                sums(i, nc.gpsimd, 0, 4, (0,))
             if i > 1:
                 back(i - 1, 0)
             back(i - 1, 1)

@@ -21,6 +21,7 @@ NG = 4
 ROWS = 256
 NPAIR = 8
 HALF = 64
+GP_HI = 2
 
 
 def tile_attention_pa_kernel(tc, query, wq, bq, cos, sin, out_0, out_1):
@@ -173,14 +174,15 @@ def tile_attention_pa_kernel(tc, query, wq, bq, cos, sin, out_0, out_1):
             for f in halves:
                 eng.tensor_tensor(out=prods[(i, 2 * f)][:, P * b0 : P * b1], in0=prods[(i, 2 * f)][:, P * b0 : P * b1],
                                   in1=prods[(i, 2 * f + 1)][:, P * b0 : P * b1], op=ALU.add)
-                summed[(i, f)] = True
+                for b in range(b0, b1):
+                    summed[(i, f, b)] = True
 
         def back(i, bp):
             ob = obp.tile([P, 512], F32, name="ob", tag="ob")
             for f in range(2):
-                nt = 1 if (i, f) in summed else 2
                 for bl in range(2):
                     b = 2 * bp + bl
+                    nt = 1 if (i, f, b) in summed else 2
                     c0 = ROWS * f + P * bl
                     for t in range(nt):
                         nc.tensor.matmul(out=ob[:, c0 : c0 + P], lhsT=prods[(i, 2 * f + t)][:, P * b : P * (b + 1)], rhs=identf[:],
@@ -306,6 +308,7 @@ def tile_attention_pa_kernel(tc, query, wq, bq, cos, sin, out_0, out_1):
             else:
                 products(i, 0, 4)
                 sums(i, nc.gpsimd, 0, 4, (0,))
+                sums(i, nc.gpsimd, 0, GP_HI, (1,))
             if i > 1:
                 back(i - 1, 0)
             back(i - 1, 1)

@@ -168,6 +168,16 @@ def tile_attention_pa_kernel(tc, query, wq, bq, cos, sin, out_0, out_1):
             for k in ((0, 1, 3, 2) if 0 < i < NPAIR - 1 else (0, 3, 1, 2)):
                 product(i, k, b0, b1)
 
+        def high_bank_products(i):
+            th = prod.tile([P, 512], F32, name="th", tag="th")
+            nc.scalar.activation(out=th[:], in_=accs[(i, 1)][:], func=ACT.Identity, bias=bt[:, NPAIR + i : NPAIR + i + 1], scale=1.0)
+            for k in (1, 2):
+                pt = prod.tile([P, 512], F32, name="pt" + str(k), tag="pt" + str(k))
+                prods[(i, k)] = pt
+                nc.gpsimd.tensor_tensor(
+                    out=pt[:].rearrange("p (b s) -> p b s", s=S), in0=th[:].rearrange("p (b s) -> p b s", s=S),
+                    in1=tabs[:, k, :].unsqueeze(1).to_broadcast([P, B, S]), op=ALU.mult)
+
         summed = {}
 
         def sums(i, eng, b0, b1, halves=(0, 1)):
@@ -305,6 +315,10 @@ def tile_attention_pa_kernel(tc, query, wq, bq, cos, sin, out_0, out_1):
                         matmuls(i, f, bp)
             if last:
                 products(i, 0, 2)
+            elif i == NPAIR - 2:
+                high_bank_products(i)
+                product(i, 0, 0, 4)
+                product(i, 3, 0, 4)
             else:
                 products(i, 0, 4)
                 sums(i, nc.gpsimd, 0, 4, (0,))

@@ -34,6 +34,7 @@ def tile_attention_pa_kernel(tc, query, wq, bq, cos, sin, out_0, out_1):
         wcp = ctx.enter_context(tc.tile_pool(name="wcp", bufs=4))
         prod = ctx.enter_context(tc.tile_pool(name="prod", bufs=2))
         work = ctx.enter_context(tc.tile_pool(name="work", bufs=4))
+        dip = ctx.enter_context(tc.tile_pool(name="dip", bufs=4))
         tpp = ctx.enter_context(tc.psum_pool(name="tpp", bufs=4))
         accp = ctx.enter_context(tc.psum_pool(name="accp", bufs=2))
         obp = ctx.enter_context(tc.psum_pool(name="obp", bufs=2))
@@ -99,6 +100,13 @@ def tile_attention_pa_kernel(tc, query, wq, bq, cos, sin, out_0, out_1):
             nc.vector.tensor_copy(out=bt[:], in_=small[:, 4, 0 : 2 * NPAIR])
 
         groupeds, codes = {}, {}
+        sorted_words = {}
+
+        def sort_words(key, j):
+            t = dip.tile([P, DIM // 2], F32, name="sw", tag="sw")
+            nc.vector.tensor_copy(out=t[:].rearrange("p (g u q) -> p g u q", g=NG, u=2),
+                                  in_=raws[(key, j)][:].bitcast(F32).rearrange("p (g q u) -> p g u q", g=NG, u=2))
+            sorted_words[(key, j)] = t
 
         def transposes(key, j):
             if j == 0:
@@ -112,7 +120,10 @@ def tile_attention_pa_kernel(tc, query, wq, bq, cos, sin, out_0, out_1):
                     for u in range(2):
                         base = 256 * (2 * gh + gl)
                         slot = 2 * gl + u if key[0] == "q" else 2 * u + gl
-                        nc.tensor.transpose(tp[:, slot, :], words[:, base + u : base + 256 : 2], identf[:])
+                        if (key, j) in sorted_words:
+                            nc.tensor.transpose(tp[:, slot, :], sorted_words[(key, j)][:, base + P * u : base + P * (u + 1)], identf[:])
+                        else:
+                            nc.tensor.transpose(tp[:, slot, :], words[:, base + u : base + 256 : 2], identf[:])
                 if key[0] == "q":
                     nc.scalar.copy(
                         out=gwords.rearrange("p (g r u) -> p g r u", g=NG, u=2)[:, 2 * gh : 2 * gh + 2, P * j : P * (j + 1), :],
@@ -288,6 +299,8 @@ def tile_attention_pa_kernel(tc, query, wq, bq, cos, sin, out_0, out_1):
         sums(0, nc.vector, 0, 2)
         quantize(q1, 0, 2)
         quantize(q1, 2, 4)
+        sort_words(w(2), 0)
+        sort_words(w(2), 1)
         transposes(w(1), 0)
         keep_warm(1)
         transposes(w(1), 1)

@@ -30,7 +30,6 @@ def tile_attention_pa_kernel(tc, query, wq, bq, cos, sin, out_0, out_1):
         const = ctx.enter_context(tc.tile_pool(name="const", bufs=1))
         rawp = ctx.enter_context(tc.tile_pool(name="rawp", bufs=20))
         grp = ctx.enter_context(tc.tile_pool(name="grp", bufs=3))
-        qcp = ctx.enter_context(tc.tile_pool(name="qcp", bufs=2))
         wcp = ctx.enter_context(tc.tile_pool(name="wcp", bufs=4))
         prod = ctx.enter_context(tc.tile_pool(name="prod", bufs=2))
         work = ctx.enter_context(tc.tile_pool(name="work", bufs=4))
@@ -133,11 +132,20 @@ def tile_attention_pa_kernel(tc, query, wq, bq, cos, sin, out_0, out_1):
                         out=gwords.rearrange("p (gh y hl j u) -> p gh y hl j u", gh=2, y=4, hl=2, u=2)[:, gh, :, j, :, :],
                         in_=tp[:].rearrange("p q r -> p (q r)").rearrange("p (u y j) -> p y j u", u=2, y=4))
 
+        qcd = const.tile([P, NG * 2 * ROWS], U32, name="qcd", align_bytes=64)
+        qsc = const.tile([P, NG * 2 * ROWS], U8, name="qsc", align_bytes=64)
+
         def quantize(key, lo, hi):
+            if key[0] == "q":
+                for g in range(lo, hi):
+                    c0 = (2 * g + key[1]) * ROWS
+                    nc.vector.quantize_mx(
+                        out=qcd[:, c0 : c0 + ROWS].bitcast(FP8X4), scales=qsc[:, c0 : c0 + ROWS],
+                        in_=groupeds[key][:, 4 * ROWS * g : 4 * ROWS * (g + 1)])
+                return
             if key not in codes:
-                pool = qcp if key[0] == "q" else wcp
-                cd = pool.tile([P, NG * ROWS], U32, name="cd" + key[0], tag="cd" + key[0], align_bytes=64)
-                sc = pool.tile([P, NG * ROWS], U8, name="sc" + key[0], tag="sc" + key[0], align_bytes=64)
+                cd = wcp.tile([P, NG * ROWS], U32, name="cdw", tag="cdw", align_bytes=64)
+                sc = wcp.tile([P, NG * ROWS], U8, name="scw", tag="scw", align_bytes=64)
                 codes[key] = (cd, sc)
             cd, sc = codes[key]
             nc.vector.quantize_mx(
@@ -151,14 +159,15 @@ def tile_attention_pa_kernel(tc, query, wq, bq, cos, sin, out_0, out_1):
                 acc = accp.tile([P, 512], F32, name="acc", tag="acc")
                 accs[(i, f)] = acc
             acc = accs[(i, f)]
-            qc, qs = codes[("q", bp)]
             wc, ws = codes[("w", i)]
+            n0, n1 = (0, 2 * ROWS) if bp is None else (ROWS * bp, ROWS * (bp + 1))
             for g in range(NG):
                 m0 = g * ROWS + f * P
+                c0 = 2 * g * ROWS
                 nc.tensor.matmul_mx(
-                    out=acc[:, ROWS * bp : ROWS * (bp + 1)],
+                    out=acc[:, n0:n1],
                     lhsT=wc[:, m0 : m0 + P].bitcast(FP8X4), lhsT_scale=ws[:, m0 : m0 + P],
-                    rhs=qc[:, g * ROWS : (g + 1) * ROWS].bitcast(FP8X4), rhs_scale=qs[:, g * ROWS : (g + 1) * ROWS],
+                    rhs=qcd[:, c0 + n0 : c0 + n1].bitcast(FP8X4), rhs_scale=qsc[:, c0 + n0 : c0 + n1],
                     start=(g == 0), stop=(g == NG - 1))
 
         SIDE = (0, 1, 1, 0)
@@ -324,8 +333,7 @@ def tile_attention_pa_kernel(tc, query, wq, bq, cos, sin, out_0, out_1):
                         matmuls(i, f, bp)
             else:
                 for f in range(2):
-                    for bp in range(2):
-                        matmuls(i, f, bp)
+                    matmuls(i, f, None)
             if last:
                 products(i, 0, 2)
             elif i == NPAIR - 2:

@@ -22,6 +22,7 @@ ROWS = 256
 NPAIR = 8
 HALF = 64
 GP_HI = 2
+NB = 64
 
 
 def tile_attention_pa_kernel(tc, query, wq, bq, cos, sin, out_0, out_1):
@@ -98,6 +99,9 @@ def tile_attention_pa_kernel(tc, query, wq, bq, cos, sin, out_0, out_1):
             nc.vector.tensor_copy(out=tabs[:], in_=small[:, 0:4, :])
             nc.vector.tensor_copy(out=bt[:], in_=small[:, 4, 0 : 2 * NPAIR])
 
+        def bridge(cols):
+            nc.tensor.matmul(out=cols, lhsT=dz[:, 0:P], rhs=dz[:, 0:NB], start=True, stop=True)
+
         groupeds, codes = {}, {}
         sorted_words = {}
 
@@ -107,7 +111,7 @@ def tile_attention_pa_kernel(tc, query, wq, bq, cos, sin, out_0, out_1):
                                   in_=raws[(key, j)][:].bitcast(F32).rearrange("p (g q u) -> p g u q", g=NG, u=2))
             sorted_words[(key, j)] = t
 
-        def transposes(key, j):
+        def transposes(key, j, lead=False):
             if j == 0:
                 grouped = grp.tile([P, NG * ROWS * 4], BF16, name="grouped", tag="grouped", align_bytes=64)
                 groupeds[key] = grouped
@@ -115,6 +119,8 @@ def tile_attention_pa_kernel(tc, query, wq, bq, cos, sin, out_0, out_1):
             gwords = groupeds[key][:].bitcast(F32)
             for gh in range(2):
                 tp = tpp.tile([P, 4, P], F32, name="tp", tag="tp")
+                if lead and gh == 0:
+                    bridge(tp[:, 0, 0:NB])
                 for gl in range(2):
                     for u in range(2):
                         base = 256 * (2 * gh + gl)
@@ -154,13 +160,17 @@ def tile_attention_pa_kernel(tc, query, wq, bq, cos, sin, out_0, out_1):
 
         accs, prods, obs, outs, rcs = {}, {}, {}, {}, {}
 
-        def matmuls(i, f, bp):
+
+        def matmuls(i, f, bp, lead=False):
             if (i, f) not in accs:
                 acc = accp.tile([P, 512], F32, name="acc", tag="acc")
                 accs[(i, f)] = acc
             acc = accs[(i, f)]
+
             wc, ws = codes[("w", i)]
             n0, n1 = (0, 2 * ROWS) if bp is None else (ROWS * bp, ROWS * (bp + 1))
+            if lead:
+                bridge(acc[:, n0 : n0 + NB])
             for g in range(NG):
                 m0 = g * ROWS + f * P
                 c0 = 2 * g * ROWS
@@ -207,8 +217,10 @@ def tile_attention_pa_kernel(tc, query, wq, bq, cos, sin, out_0, out_1):
                 for b in range(b0, b1):
                     summed[(i, f, b)] = True
 
-        def back(i, bp):
+        def back(i, bp, lead=False):
             ob = obp.tile([P, 512], F32, name="ob", tag="ob")
+            if lead:
+                bridge(ob[:, 0:NB])
             for f in range(2):
                 for bl in range(2):
                     b = 2 * bp + bl
@@ -300,9 +312,9 @@ def tile_attention_pa_kernel(tc, query, wq, bq, cos, sin, out_0, out_1):
         quantize(q0, 0, 2)
         quantize(q0, 2, 4)
         transposes(q1, 0)
-        matmuls(0, 0, 0)
+        matmuls(0, 0, 0, True)
         matmuls(0, 1, 0)
-        transposes(q1, 1)
+        transposes(q1, 1, True)
         keep_warm(1)
         products(0, 0, 2)
         sums(0, nc.vector, 0, 2)
@@ -313,9 +325,9 @@ def tile_attention_pa_kernel(tc, query, wq, bq, cos, sin, out_0, out_1):
         transposes(w(1), 0)
         keep_warm(1)
         transposes(w(1), 1)
-        matmuls(0, 0, 1)
+        matmuls(0, 0, 1, True)
         matmuls(0, 1, 1)
-        back(0, 0)
+        back(0, 0, True)
         quantize(w(1), 0, NG)
         products(0, 2, 4)
         sums(0, nc.vector, 2, 4)
@@ -330,10 +342,10 @@ def tile_attention_pa_kernel(tc, query, wq, bq, cos, sin, out_0, out_1):
             if last:
                 for bp in range(2):
                     for f in range(2):
-                        matmuls(i, f, bp)
+                        matmuls(i, f, bp, (bp, f) == (0, 0))
             else:
                 for f in range(2):
-                    matmuls(i, f, None)
+                    matmuls(i, f, None, f == 0)
             if last:
                 products(i, 0, 2)
             elif i == NPAIR - 2:
@@ -345,8 +357,8 @@ def tile_attention_pa_kernel(tc, query, wq, bq, cos, sin, out_0, out_1):
                 sums(i, nc.gpsimd, 0, 4, (0,))
                 sums(i, nc.gpsimd, 0, GP_HI, (1,))
             if i > 1:
-                back(i - 1, 0)
-            back(i - 1, 1)
+                back(i - 1, 0, True)
+            back(i - 1, 1, i == 1)
             if last:
                 products(i, 2, 4)
             if i + 2 < NPAIR:

@@ -22,7 +22,6 @@ ROWS = 256
 NPAIR = 8
 HALF = 64
 GP_HI = 2
-NB = 64
 
 
 def tile_attention_pa_kernel(tc, query, wq, bq, cos, sin, out_0, out_1):
@@ -99,9 +98,6 @@ def tile_attention_pa_kernel(tc, query, wq, bq, cos, sin, out_0, out_1):
             nc.vector.tensor_copy(out=tabs[:], in_=small[:, 0:4, :])
             nc.vector.tensor_copy(out=bt[:], in_=small[:, 4, 0 : 2 * NPAIR])
 
-        def bridge(cols):
-            nc.tensor.matmul(out=cols, lhsT=dz[:, 0:P], rhs=dz[:, 0:NB], start=True, stop=True)
-
         groupeds, codes = {}, {}
         sorted_words = {}
 
@@ -119,8 +115,6 @@ def tile_attention_pa_kernel(tc, query, wq, bq, cos, sin, out_0, out_1):
             gwords = groupeds[key][:].bitcast(F32)
             for gh in range(2):
                 tp = tpp.tile([P, 4, P], F32, name="tp", tag="tp")
-                if lead and gh == 0:
-                    bridge(tp[:, 0, 0:NB])
                 for gl in range(2):
                     for u in range(2):
                         base = 256 * (2 * gh + gl)
@@ -169,8 +163,6 @@ def tile_attention_pa_kernel(tc, query, wq, bq, cos, sin, out_0, out_1):
 
             wc, ws = codes[("w", i)]
             n0, n1 = (0, 2 * ROWS) if bp is None else (ROWS * bp, ROWS * (bp + 1))
-            if lead:
-                bridge(acc[:, n0 : n0 + NB])
             for g in range(NG):
                 m0 = g * ROWS + f * P
                 c0 = 2 * g * ROWS
@@ -219,8 +211,6 @@ def tile_attention_pa_kernel(tc, query, wq, bq, cos, sin, out_0, out_1):
 
         def back(i, bp, lead=False):
             ob = obp.tile([P, 512], F32, name="ob", tag="ob")
-            if lead:
-                bridge(ob[:, 0:NB])
             for f in range(2):
                 for bl in range(2):
                     b = 2 * bp + bl

@@ -34,9 +34,8 @@ def tile_attention_pa_kernel(tc, query, wq, bq, cos, sin, out_0, out_1):
         prod = ctx.enter_context(tc.tile_pool(name="prod", bufs=2))
         work = ctx.enter_context(tc.tile_pool(name="work", bufs=4))
         dip = ctx.enter_context(tc.tile_pool(name="dip", bufs=4))
-        tpp = ctx.enter_context(tc.psum_pool(name="tpp", bufs=4))
-        accp = ctx.enter_context(tc.psum_pool(name="accp", bufs=2))
-        obp = ctx.enter_context(tc.psum_pool(name="obp", bufs=2))
+        tpp = ctx.enter_context(tc.psum_pool(name="tpp", bufs=5))
+        accp = ctx.enter_context(tc.psum_pool(name="accp", bufs=3))
         ctx.enter_context(tc.manual_schedule())
 
         zeros = const.tile([P, 1], F32, name="zeros")
@@ -210,7 +209,7 @@ def tile_attention_pa_kernel(tc, query, wq, bq, cos, sin, out_0, out_1):
                     summed[(i, f, b)] = True
 
         def back(i, bp, lead=False):
-            ob = obp.tile([P, 512], F32, name="ob", tag="ob")
+            ob = tpp.tile([P, 512], F32, name="tp", tag="tp")
             for f in range(2):
                 for bl in range(2):
                     b = 2 * bp + bl
@@ -278,7 +277,7 @@ def tile_attention_pa_kernel(tc, query, wq, bq, cos, sin, out_0, out_1):
                         in_=f8[:, ROWS * bl : ROWS * (bl + 1)].bitcast(U8).rearrange("p (h d) -> p h d", d=HD))
 
         q0, q1 = ("q", 0), ("q", 1)
-        dm = obp.tile([P, 512], F32, name="ob", tag="ob")
+        dm = accp.tile([P, 512], F32, name="acc", tag="acc")
 
         def keep_warm(n):
             for r in range(n):

from contextlib import ExitStack

import concourse.mybir as mybir
from concourse.masks import make_identity

B, S, DIM, H, HD = 4, 128, 2048, 16, 128
FLOPS = 2 * B * S * DIM * H * HD

F32 = mybir.dt.float32
BF16 = mybir.dt.bfloat16
U32 = mybir.dt.uint32
U8 = mybir.dt.uint8
FP8X4 = mybir.dt.float8_e4m3fn_x4
FP8 = mybir.dt.float8_e4m3fn
ALU = mybir.AluOpType
ACT = mybir.ActivationFunctionType
AX = mybir.AxisListType

P = 128
NG = 4
ROWS = 256
NPAIR = 8
HALF = 64
GP_HI = 2


def tile_attention_pa_kernel(tc, query, wq, bq, cos, sin, out_0, out_1):
    nc = tc.nc
    with ExitStack() as ctx:
        const = ctx.enter_context(tc.tile_pool(name="const", bufs=1))
        rawp = ctx.enter_context(tc.tile_pool(name="rawp", bufs=20))
        grp = ctx.enter_context(tc.tile_pool(name="grp", bufs=3))
        wcp = ctx.enter_context(tc.tile_pool(name="wcp", bufs=4))
        prod = ctx.enter_context(tc.tile_pool(name="prod", bufs=2))
        work = ctx.enter_context(tc.tile_pool(name="work", bufs=4))
        dip = ctx.enter_context(tc.tile_pool(name="dip", bufs=4))
        tpp = ctx.enter_context(tc.psum_pool(name="tpp", bufs=5))
        accp = ctx.enter_context(tc.psum_pool(name="accp", bufs=3))
        ctx.enter_context(tc.manual_schedule())

        zeros = const.tile([P, 1], F32, name="zeros")
        nc.vector.memset(zeros[:], 0.0)
        dz = const.tile([P, 512], BF16, name="dz")
        nc.vector.memset(dz[:], 0.0)
        zb = const.tile([P, P], BF16, name="zb")
        nc.vector.memset(zb[:], 0.0)
        bq4 = bq.rearrange("(i hl f j) -> f i hl j", i=NPAIR, hl=2, f=2, j=HALF)
        cosb = const.tile([P, HD], BF16, name="cosb")
        sinb = const.tile([P, HD], BF16, name="sinb")
        warm = const.tile([P, 1], F32, name="warm")
        nc.scalar.activation(out=warm[:], in_=zeros[:], func=ACT.Identity, bias=zeros[:, 0:1], scale=zeros[:, 0:1])
        identf = const.tile([P, P], F32, name="identf")
        make_identity(nc, identf[:])
        identb = const.tile([P, P], BF16, name="identb")
        make_identity(nc, identb[:])

        order = [("w", 0), ("q", 0), ("q", 1)] + [("w", i) for i in range(1, NPAIR)]
        raws = {}
        for key in order:
            for j in range(2):
                raw = rawp.tile([P, DIM], BF16, name="raw", tag="raw")
                if key[0] == "q":
                    src = query[2 * key[1] + j]
                else:
                    src = wq[ROWS * key[1] + P * j : ROWS * key[1] + P * (j + 1), :]
                pieces = NG if (key, j) == (("w", 0), 0) else 1
                step = DIM // pieces
                for c in range(pieces):
                    nc.sync.dma_start(out=raw[:, step * c : step * (c + 1)], in_=src[:, step * c : step * (c + 1)])
                raws[(key, j)] = raw
            if key == ("q", 0):
                for f in range(2):
                    nc.sync.dma_start(out=zb[NPAIR * f : NPAIR * (f + 1), :].rearrange("p (hl j) -> p hl j", hl=2), in_=bq4[f])
                nc.sync.dma_start(out=cosb[:], in_=cos[0, 0])
                nc.sync.dma_start(out=sinb[:], in_=sin[0, 0])

        xt = const.tile([P, 4, P], BF16, name="xt")

        def dup(k, src, lo, sign):
            nc.vector.tensor_scalar(
                out=xt[:, k, :].rearrange("p (hl j) -> p hl j", hl=2),
                in0=src[:, lo : lo + HALF].unsqueeze(1).to_broadcast([P, 2, HALF]),
                scalar1=sign, scalar2=None, op0=ALU.mult)

        tabs = const.tile([P, 4, P], F32, name="tabs")
        bt = const.tile([P, 2 * NPAIR], F32, name="bt")

        def tables():
            dup(0, cosb, 0, 1.0)
            dup(1, sinb, 0, -1.0)
            dup(2, cosb, HALF, 1.0)
            dup(3, sinb, HALF, 1.0)
            small = tpp.tile([P, 5, P], BF16, name="tp", tag="tp")
            for k in range(4):
                nc.tensor.transpose(small[:, k, :], xt[:, k, :], identb[:])
            nc.tensor.transpose(small[:, 4, :], zb[:], identb[:])
            nc.vector.tensor_copy(out=tabs[:], in_=small[:, 0:4, :])
            nc.vector.tensor_copy(out=bt[:], in_=small[:, 4, 0 : 2 * NPAIR])

        groupeds, codes = {}, {}
        sorted_words = {}

        def sort_words(key, j):
            t = dip.tile([P, DIM // 2], F32, name="sw", tag="sw")
            nc.vector.tensor_copy(out=t[:].rearrange("p (g u q) -> p g u q", g=NG, u=2),
                                  in_=raws[(key, j)][:].bitcast(F32).rearrange("p (g q u) -> p g u q", g=NG, u=2))
            sorted_words[(key, j)] = t

        def transposes(key, j, lead=False):
            if j == 0:
                grouped = grp.tile([P, NG * ROWS * 4], BF16, name="grouped", tag="grouped", align_bytes=64)
                groupeds[key] = grouped
            words = raws[(key, j)][:].bitcast(F32)
            gwords = groupeds[key][:].bitcast(F32)
            for gh in range(2):
                tp = tpp.tile([P, 4, P], F32, name="tp", tag="tp")
                for gl in range(2):
                    for u in range(2):
                        base = 256 * (2 * gh + gl)
                        slot = 2 * gl + u if key[0] == "q" else 2 * u + gl
                        if (key, j) in sorted_words:
                            nc.tensor.transpose(tp[:, slot, :], sorted_words[(key, j)][:, base + P * u : base + P * (u + 1)], identf[:])
                        else:
                            nc.tensor.transpose(tp[:, slot, :], words[:, base + u : base + 256 : 2], identf[:])
                if key[0] == "q":
                    nc.scalar.copy(
                        out=gwords.rearrange("p (g r u) -> p g r u", g=NG, u=2)[:, 2 * gh : 2 * gh + 2, P * j : P * (j + 1), :],
                        in_=tp[:].rearrange("p (gl u) r -> p gl r u", u=2))
                else:
                    nc.scalar.copy(
                        out=gwords.rearrange("p (gh y hl j u) -> p gh y hl j u", gh=2, y=4, hl=2, u=2)[:, gh, :, j, :, :],
                        in_=tp[:].rearrange("p q r -> p (q r)").rearrange("p (u y j) -> p y j u", u=2, y=4))

        qcd = const.tile([P, NG * 2 * ROWS], U32, name="qcd", align_bytes=64)
        qsc = const.tile([P, NG * 2 * ROWS], U8, name="qsc", align_bytes=64)

        def quantize(key, lo, hi):
            if key[0] == "q":
                for g in range(lo, hi):
                    c0 = (2 * g + key[1]) * ROWS
                    nc.vector.quantize_mx(
                        out=qcd[:, c0 : c0 + ROWS].bitcast(FP8X4), scales=qsc[:, c0 : c0 + ROWS],
                        in_=groupeds[key][:, 4 * ROWS * g : 4 * ROWS * (g + 1)])
                return
            if key not in codes:
                cd = wcp.tile([P, NG * ROWS], U32, name="cdw", tag="cdw", align_bytes=64)
                sc = wcp.tile([P, NG * ROWS], U8, name="scw", tag="scw", align_bytes=64)
                codes[key] = (cd, sc)
            cd, sc = codes[key]
            nc.vector.quantize_mx(
                out=cd[:, ROWS * lo : ROWS * hi].bitcast(FP8X4), scales=sc[:, ROWS * lo : ROWS * hi],
                in_=groupeds[key][:, 4 * ROWS * lo : 4 * ROWS * hi])

        accs, prods, obs, outs, rcs = {}, {}, {}, {}, {}


        def matmuls(i, f, bp, lead=False):
            if (i, f) not in accs:
                acc = accp.tile([P, 512], F32, name="acc", tag="acc")
                accs[(i, f)] = acc
            acc = accs[(i, f)]

            wc, ws = codes[("w", i)]
            n0, n1 = (0, 2 * ROWS) if bp is None else (ROWS * bp, ROWS * (bp + 1))
            for g in range(NG):
                m0 = g * ROWS + f * P
                c0 = 2 * g * ROWS
                nc.tensor.matmul_mx(
                    out=acc[:, n0:n1],
                    lhsT=wc[:, m0 : m0 + P].bitcast(FP8X4), lhsT_scale=ws[:, m0 : m0 + P],
                    rhs=qcd[:, c0 + n0 : c0 + n1].bitcast(FP8X4), rhs_scale=qsc[:, c0 + n0 : c0 + n1],
                    start=(g == 0), stop=(g == NG - 1))

        SIDE = (0, 1, 1, 0)

        def product(i, k, b0, b1):
            if (i, k) not in prods:
                pt = prod.tile([P, 512], F32, name="pt" + str(k), tag="pt" + str(k))
                prods[(i, k)] = pt
            f = SIDE[k]
            nc.vector.scalar_tensor_tensor(
                out=prods[(i, k)][:, P * b0 : P * b1].rearrange("p (b s) -> p b s", s=S),
                in0=accs[(i, f)][:, P * b0 : P * b1].rearrange("p (b s) -> p b s", s=S),
                scalar=bt[:, NPAIR * f + i : NPAIR * f + i + 1],
                in1=tabs[:, k, :].unsqueeze(1).to_broadcast([P, b1 - b0, S]),
                op0=ALU.add, op1=ALU.mult)

        def products(i, b0, b1):
            for k in ((0, 1, 3, 2) if 0 < i < NPAIR - 1 else (0, 3, 1, 2)):
                product(i, k, b0, b1)

        def high_bank_products(i):
            th = prod.tile([P, 512], F32, name="th", tag="th")
            nc.scalar.activation(out=th[:], in_=accs[(i, 1)][:], func=ACT.Identity, bias=bt[:, NPAIR + i : NPAIR + i + 1], scale=1.0)
            for k in (1, 2):
                pt = prod.tile([P, 512], F32, name="pt" + str(k), tag="pt" + str(k))
                prods[(i, k)] = pt
                nc.gpsimd.tensor_tensor(
                    out=pt[:].rearrange("p (b s) -> p b s", s=S), in0=th[:].rearrange("p (b s) -> p b s", s=S),
                    in1=tabs[:, k, :].unsqueeze(1).to_broadcast([P, B, S]), op=ALU.mult)

        summed = {}

        def sums(i, eng, b0, b1, halves=(0, 1)):
            for f in halves:
                eng.tensor_tensor(out=prods[(i, 2 * f)][:, P * b0 : P * b1], in0=prods[(i, 2 * f)][:, P * b0 : P * b1],
                                  in1=prods[(i, 2 * f + 1)][:, P * b0 : P * b1], op=ALU.add)
                for b in range(b0, b1):
                    summed[(i, f, b)] = True

        def back(i, bp, lead=False):
            ob = tpp.tile([P, 512], F32, name="tp", tag="tp")
            for f in range(2):
                for bl in range(2):
                    b = 2 * bp + bl
                    nt = 1 if (i, f, b) in summed else 2
                    c0 = ROWS * f + P * bl
                    for t in range(nt):
                        nc.tensor.matmul(out=ob[:, c0 : c0 + P], lhsT=prods[(i, 2 * f + t)][:, P * b : P * (b + 1)], rhs=identf[:],
                                         is_transpose=True, start=(t == 0), stop=(t == nt - 1))
            o = work.tile([P, 512], F32, name="o", tag="o", bufs=5)
            nc.scalar.copy(out=o[:].rearrange("p (x f j) -> p x f j", f=2, j=HALF),
                           in_=ob[:].rearrange("p (f x j) -> p x f j", f=2, j=HALF))
            outs[(i, bp)] = o
            for bl in range(2):
                nc.sync.dma_start(
                    out=out_0[2 * bp + bl, 2 * i : 2 * i + 2].rearrange("h s d -> s h d"),
                    in_=o[:, ROWS * bl : ROWS * (bl + 1)].rearrange("p (h d) -> p h d", d=HD))

        def bytes_out(i, bp, shared=False):
            o = outs[(i, bp)]
            am = work.tile([P, 4], F32, name="am", tag="am")
            nc.vector.tensor_reduce(out=am[:], in_=o[:].rearrange("p (x d) -> p x d", d=HD), axis=AX.X, op=ALU.max,
                                    apply_absolute_value=True)
            rc = work.tile([P, 4], F32, name="rc", tag="rc")
            nc.vector.reciprocal(out=rc[:], in_=am[:])
            rs = work.tile([P, 4], F32, name="rs", tag="rs")
            if shared:
                nc.vector.tensor_scalar(out=rs[:], in0=rc[:], scalar1=448.0, scalar2=None, op0=ALU.mult)
            else:
                nc.scalar.activation(out=rs[:], in_=rc[:], func=ACT.Copy, scale=448.0)
            f8 = work.tile([P, 512], FP8, name="f8", tag="f8")
            for x in range(4):
                if shared and x < 3:
                    nc.vector.tensor_scalar(out=f8[:, HD * x : HD * (x + 1)], in0=o[:, HD * x : HD * (x + 1)],
                                            scalar1=rs[:, x : x + 1], scalar2=None, op0=ALU.mult, saturate=False)
                else:
                    nc.scalar.activation(out=f8[:, HD * x : HD * (x + 1)], in_=o[:, HD * x : HD * (x + 1)], func=ACT.Identity,
                                         bias=zeros[:, 0:1], scale=rs[:, x : x + 1], saturate=False)
            for bl in range(2):
                nc.sync.dma_start(
                    out=out_1[2 * bp + bl, 2 * i : 2 * i + 2].rearrange("h s d -> s h d"),
                    in_=f8[:, ROWS * bl : ROWS * (bl + 1)].bitcast(U8).rearrange("p (h d) -> p h d", d=HD))

        def bytes_both(i):
            ams, rss = [], []
            for bp in range(2):
                am = work.tile([P, 4], F32, name="am", tag="am")
                nc.vector.tensor_reduce(out=am[:], in_=outs[(i, bp)][:].rearrange("p (x d) -> p x d", d=HD), axis=AX.X, op=ALU.max,
                                        apply_absolute_value=True)
                ams.append(am)
            for bp in range(2):
                rc = work.tile([P, 4], F32, name="rc", tag="rc")
                nc.vector.reciprocal(out=rc[:], in_=ams[bp][:])
                rs = work.tile([P, 4], F32, name="rs", tag="rs")
                nc.scalar.activation(out=rs[:], in_=rc[:], func=ACT.Copy, scale=448.0)
                rss.append(rs)
            for bp in range(2):
                o = outs[(i, bp)]
                f8 = work.tile([P, 512], FP8, name="f8", tag="f8")
                for x in range(4):
                    nc.scalar.activation(out=f8[:, HD * x : HD * (x + 1)], in_=o[:, HD * x : HD * (x + 1)], func=ACT.Identity,
                                         bias=zeros[:, 0:1], scale=rss[bp][:, x : x + 1], saturate=False)
                for bl in range(2):
                    nc.sync.dma_start(
                        out=out_1[2 * bp + bl, 2 * i : 2 * i + 2].rearrange("h s d -> s h d"),
                        in_=f8[:, ROWS * bl : ROWS * (bl + 1)].bitcast(U8).rearrange("p (h d) -> p h d", d=HD))

        q0, q1 = ("q", 0), ("q", 1)
        dm = accp.tile([P, 512], F32, name="acc", tag="acc")

        def keep_warm(n):
            for r in range(n):
                nc.tensor.matmul(out=dm[:], lhsT=dz[:, 0:P], rhs=dz[:], start=True, stop=True)

        def w(i):
            return ("w", i)

        keep_warm(4)
        transposes(w(0), 0)
        keep_warm(1)
        transposes(w(0), 1)
        keep_warm(1)
        transposes(q0, 0)
        keep_warm(1)
        quantize(w(0), 0, 2)
        quantize(w(0), 2, 4)
        transposes(q0, 1)
        keep_warm(1)
        tables()
        quantize(q0, 0, 2)
        quantize(q0, 2, 4)
        transposes(q1, 0)
        matmuls(0, 0, 0, True)
        matmuls(0, 1, 0)
        transposes(q1, 1, True)
        keep_warm(1)
        products(0, 0, 2)
        sums(0, nc.vector, 0, 2)
        quantize(q1, 0, 2)
        quantize(q1, 2, 4)
        sort_words(w(2), 0)
        sort_words(w(2), 1)
        transposes(w(1), 0)
        keep_warm(1)
        transposes(w(1), 1)
        matmuls(0, 0, 1, True)
        matmuls(0, 1, 1)
        back(0, 0, True)
        quantize(w(1), 0, NG)
        products(0, 2, 4)
        sums(0, nc.vector, 2, 4)
        transposes(w(2), 0)
        transposes(w(2), 1)
        bytes_out(0, 0)

        for i in range(1, NPAIR):
            last = i == NPAIR - 1
            if not last:
                quantize(w(i + 1), 0, NG)
            if last:
                for bp in range(2):
                    for f in range(2):
                        matmuls(i, f, bp, (bp, f) == (0, 0))
            else:
                for f in range(2):
                    matmuls(i, f, None, f == 0)
            if last:
                products(i, 0, 2)
            elif i == NPAIR - 2:
                high_bank_products(i)
                product(i, 0, 0, 4)
                product(i, 3, 0, 4)
            else:
                products(i, 0, 4)
                sums(i, nc.gpsimd, 0, 4, (0,))
                sums(i, nc.gpsimd, 0, GP_HI, (1,))
            if i > 1:
                back(i - 1, 0, True)
            back(i - 1, 1, i == 1)
            if last:
                products(i, 2, 4)
            if i + 2 < NPAIR:
                transposes(w(i + 2), 0)
                transposes(w(i + 2), 1)
            if last:
                back(i, 0)
                back(i, 1)
            if i > 1:
                bytes_both(i - 1)
            else:
                bytes_out(i - 1, 1)
        bytes_out(NPAIR - 1, 0)
        bytes_out(NPAIR - 1, 1, True)
